import numpy as np
import ml_dtypes


def mxq(x, axis, fmt="e4m3"):
    dtype, down = {"e4m3": (ml_dtypes.float8_e4m3fn, 7), "e5m2": (ml_dtypes.float8_e5m2, 14)}[fmt]
    v = np.moveaxis(np.asarray(x, np.float32).astype(ml_dtypes.bfloat16).astype(np.float64), axis, -1)
    blocks = v.reshape(v.shape[:-1] + (-1, 32))
    amax = np.abs(blocks).max(-1, keepdims=True)
    byte = np.maximum(np.where(amax > 0, np.frexp(amax)[1] - 1 + 127, 0) - down, 1)
    scale = np.exp2(byte - 127.0)
    codes = (blocks / scale).astype(np.float32).astype(dtype).astype(np.float64)
    return np.moveaxis((codes * scale).reshape(v.shape), -1, axis)


WIDE = False


def mx_kscale(k):
    if not WIDE:
        return np.ones(k)
    levels = np.array([10, -10, 5, -5, 0])
    if k % 512:
        return np.exp2(np.random.permutation(np.resize(levels, k // 32))).repeat(32)
    a = np.empty((k // 512, 16))
    for p in range(k // 512):
        a[p, :8] = np.random.permutation(np.resize(levels, 8))
        for g in range(8):
            far = levels[np.abs(levels - a[p, g]) >= 10]
            a[p, g + 8] = far[np.random.randint(len(far))]
    return np.exp2(a.ravel()).repeat(32)


BF16 = ml_dtypes.bfloat16


def bf(x):
    return np.asarray(x, np.float32).astype(BF16)


def f64(x):
    return np.asarray(x).astype(np.float64)


N, DK, DV = 4096, 128, 128


def setup_inputs():
    s = mx_kscale(N)
    q = np.random.standard_normal((N, DK)) * 1.4
    k = np.random.standard_normal((N, DK)) * 1.4
    v = np.random.standard_normal((N, DV)) * 2.0
    q[:, 0] = 8.0
    k[:, 0] += np.log(s) * np.sqrt(DK) / 8.0
    v = v * np.mean(s) / s[:, None]
    return {"q": bf(q), "k": bf(k), "v": bf(v)}


def reference(q, k, v):
    scores = f64(q) @ f64(k).T / np.sqrt(DK)
    scores = scores + np.triu(np.ones((N, N)), k=1)
    e = np.exp(scores - scores.max(-1, keepdims=True))
    return (mxq(e, 1, "e4m3") @ mxq(f64(v), 0, "e4m3")) / e.sum(-1, keepdims=True)

@@ -1,0 +1,337 @@
+import math
+from contextlib import ExitStack
+
+import concourse.mybir as mybir
+from concourse.masks import make_identity
+
+F32 = mybir.dt.float32
+BF16 = mybir.dt.bfloat16
+U32 = mybir.dt.uint32
+U8 = mybir.dt.uint8
+FP8X4 = mybir.dt.float8_e4m3fn_x4
+ALU = mybir.AluOpType
+ACT = mybir.ActivationFunctionType
+
+P = 128
+N = 4096
+D = 128
+NT = N // P
+BANK = 512
+NB = N // BANK
+FLOPS = 2 * N * N * (D + D)
+
+ROOT = math.sqrt(128.0)
+SCALE = 1.0 / ROOT
+ROOT_PIECES = (11.3125, 0.0012054443359375, 3.0547380447387695e-06)
+assert abs(sum(ROOT_PIECES) - ROOT) < 1e-10
+Q_REST = ((1, 8), (8, 16), (16, 24), (24, 32))
+
+
+def tile_scaled_dot_product_kernel(tc, q, k, v, out):
+    nc = tc.nc
+    with ExitStack() as ctx:
+        const = ctx.enter_context(tc.tile_pool(name="const", bufs=1))
+        stash_pool = ctx.enter_context(tc.tile_pool(name="stash", bufs=3))
+        e_pool = ctx.enter_context(tc.tile_pool(name="e", bufs=3))
+        grouped_pool = ctx.enter_context(tc.tile_pool(name="grouped", bufs=3))
+        work = ctx.enter_context(tc.tile_pool(name="work", bufs=2))
+        small = ctx.enter_context(tc.tile_pool(name="small", bufs=6))
+        ps_s = ctx.enter_context(tc.psum_pool(name="ps_s", bufs=4))
+        ps_t = ctx.enter_context(tc.psum_pool(name="ps_t", bufs=3))
+        ps_o = ctx.enter_context(tc.psum_pool(name="ps_o", bufs=1))
+        ctx.enter_context(tc.manual_schedule())
+
+        q_raw = const.tile([P, NT, D], BF16)
+        k_raw = const.tile([P, NB, 4 * D], BF16)
+        v_raw = const.tile([P, NB, 4 * D], BF16)
+        q_view = q.rearrange("(j p) d -> p j d", p=P)
+        k_view = k.rearrange("(g p t) d -> p g (t d)", p=P, t=4)
+        v_view = v.rearrange("(g p t) d -> p g (t d)", p=P, t=4)
+        nc.sync.dma_start(out=q_raw[:, 0:1, :], in_=q_view[:, 0:1, :])
+        for g in range(NB):
+            nc.sync.dma_start(out=k_raw[:, g : g + 1, :], in_=k_view[:, g : g + 1, :])
+        for j0, j1 in Q_REST:
+            nc.sync.dma_start(out=q_raw[:, j0:j1, :], in_=q_view[:, j0:j1, :])
+        nc.sync.dma_start(out=v_raw[:], in_=v_view)
+
+        warm = const.tile([P, 2], F32)
+        nc.vector.memset(warm[:, 0:1], 0.0)
+        nc.scalar.activation(out=warm[:, 1:2], in_=warm[:, 0:1], func=ACT.Exp)
+        ident = const.tile([P, P], BF16)
+        make_identity(nc, ident[:])
+        upper = const.tile([P, P], F32)
+        nc.gpsimd.memset(upper[:], 0.0)
+        nc.gpsimd.affine_select(
+            out=upper[:],
+            in_=upper[:],
+            compare_op=ALU.is_ge,
+            fill=1.0,
+            base=0,
+            pattern=[[-1, P]],
+            channel_multiplier=1,
+        )
+        ident_f = const.tile([P, P], F32)
+        make_identity(nc, ident_f[:])
+        tri = []
+        for i in range(3):
+            m_i = const.tile([P, P], BF16, name="tri%d" % i)
+            nc.vector.tensor_scalar(
+                out=m_i[:].rearrange("q (u p b) -> q u p b", u=2, b=2),
+                in0=upper[:].rearrange("q (p u b) -> q u p b", u=2, b=2),
+                scalar1=ROOT_PIECES[i],
+                scalar2=None,
+                op0=ALU.mult,
+            )
+            tri.append(m_i)
+
+        qT = const.tile([P, N], BF16)
+        kT = const.tile([P, N], BF16)
+        v_grouped = const.tile([P, N], BF16, align_bytes=64)
+        v_codes = const.tile([P, N // 4], U32, align_bytes=64)
+        v_scales = const.tile([P, N // 4], U8, align_bytes=64)
+        rowsums = const.tile([P, NT], F32)
+        rinvs = const.tile([P, NT], F32)
+
+        def regroup(dst, src):
+            for h in range(2):
+                nc.gpsimd.tensor_scalar(
+                    out=dst[:, 2048 * h : 2048 * h + 2048].rearrange("p (g c t) -> p g c t", g=4, t=4),
+                    in0=src[:, 2048 * h : 2048 * h + 2048].rearrange("p (g t c) -> p g c t", g=4, t=4),
+                    scalar1=1.0,
+                    scalar2=0.0,
+                    op0=ALU.mult,
+                    op1=ALU.add,
+                )
+
+        def flip_q(j0, j1):
+            tp = ps_t.tile([P, 8, P], BF16, name="tp_q", tag="tp")
+            for j in range(j0, j1):
+                nc.tensor.transpose(out=tp[:, j - j0, :], in_=q_raw[:, j, :], identity=ident[:])
+            nc.scalar.copy(
+                out=qT[:, j0 * P : j1 * P], in_=tp[:, 0 : j1 - j0, :].rearrange("p a b -> p (a b)")
+            )
+
+        def flip_k(g):
+            tp = ps_t.tile([P, 4, P], BF16, name="tp_k", tag="tp")
+            for t in range(4):
+                nc.tensor.transpose(out=tp[:, t, :], in_=k_raw[:, g, t * P : (t + 1) * P], identity=ident[:])
+            nc.scalar.copy(
+                out=kT[:, g * BANK : (g + 1) * BANK].rearrange("d (u p b) -> d u p b", u=2, b=2),
+                in_=tp[:].rearrange("d (u b) p -> d u p b", u=2),
+            )
+
+        live = {}
+
+        def scores(i, b):
+            bd, sd = i // 4, i % 4
+            k0 = b * BANK
+            lq = qT[:, i * P : (i + 1) * P]
+            if b == 0:
+                live["stash", i] = stash_pool.tile([P, N], F32, name="stash")
+                live["mparts", i] = small.tile([P, 16], F32, name="mparts")
+                live["n", i] = 0
+            bank = ps_s.tile([P, BANK], F32, name="s_ps")
+            s_ps = bank[:].rearrange("q (u x) -> q u x", u=2)
+            keys = kT[:, k0 : k0 + BANK].rearrange("d (u x) -> d u x", u=2)
+            stash = live["stash", i][:, k0 : k0 + BANK].rearrange("q (u x) -> q u x", u=2)
+            lo, hi = 64 * sd, 64 * sd + 64
+            if b != bd:
+                nc.tensor.matmul(out=bank[:], lhsT=lq, rhs=kT[:, k0 : k0 + BANK], start=True, stop=True)
+            else:
+                if sd > 0:
+                    nc.tensor.matmul(out=s_ps[:, :, 0:lo], lhsT=lq, rhs=keys[:, :, 0:lo], start=True, stop=True)
+                nc.tensor.matmul(out=s_ps[:, :, lo:hi], lhsT=lq, rhs=keys[:, :, lo:hi], start=True, stop=False)
+                for j in range(3):
+                    nc.tensor.matmul(
+                        out=s_ps[:, :, lo:hi],
+                        lhsT=ident[:],
+                        rhs=tri[j][:].rearrange("q (u x) -> q u x", u=2),
+                        start=False,
+                        stop=(j == 2),
+                    )
+                if sd < 3:
+                    nc.tensor.matmul(out=s_ps[:, :, hi:256], lhsT=lq, rhs=keys[:, :, hi:256], start=True, stop=True)
+            if b < bd:
+                parts = [(0, 256, 0.0)]
+            elif b > bd:
+                parts = [(0, 256, ROOT)]
+            else:
+                parts = [(0, hi, 0.0)]
+                if sd < 3:
+                    parts.append((hi, 256, ROOT))
+            for c0, c1, shift in parts:
+                n_parts = live["n", i]
+                nc.vector.tensor_scalar(
+                    out=stash[:, :, c0:c1],
+                    in0=s_ps[:, :, c0:c1],
+                    scalar1=shift,
+                    scalar2=None,
+                    op0=ALU.add,
+                    op1=ALU.max,
+                    accum_out=live["mparts", i][:, n_parts : n_parts + 1],
+                )
+                live["n", i] = n_parts + 1
+
+        def row_bias(i):
+            n_parts = live["n", i]
+            junk = small.tile([P, 16], F32, name="junk")
+            nbias = small.tile([P, 1], F32, name="nbias")
+            nc.vector.tensor_scalar(
+                out=junk[:, 0:n_parts],
+                in0=live["mparts", i][:, 0:n_parts],
+                scalar1=-SCALE,
+                scalar2=None,
+                op0=ALU.mult,
+                op1=ALU.min,
+                accum_out=nbias[:, 0:1],
+            )
+            live["nbias", i] = nbias
+
+        def exponentials(i, k0, k1, rowsum):
+            if k0 == 0:
+                live["e", i] = e_pool.tile([P, N], BF16, name="e_sb")
+            nc.scalar.activation(
+                out=live["e", i][:, k0:k1],
+                in_=live["stash", i][:, k0:k1],
+                func=ACT.Exp,
+                bias=live["nbias", i][:, 0:1],
+                scale=SCALE,
+                accum_out=rowsum,
+            )
+
+        def flip_e(i, c):
+            if c == 0:
+                live["grouped", i] = grouped_pool.tile([P, N], BF16, name="grouped", align_bytes=64)
+            tp = ps_t.tile([P, 4, P], F32, name="tp_e", tag="tp")
+            words = live["e", i][:].bitcast(F32)
+            for w in range(4):
+                nc.tensor.transpose(
+                    out=tp[:, w, :], in_=words[:, (4 * c + w) * P : (4 * c + w + 1) * P], identity=ident_f[:]
+                )
+            live["tp", i, c] = tp
+
+        def drain_e(i, c, copy):
+            copy(
+                out=live["grouped", i][:]
+                .bitcast(F32)[:, 512 * c : 512 * c + 512]
+                .rearrange("p (g c u) -> p g c u", g=2, u=2),
+                in_=live["tp", i, c][:].rearrange("p (g u) c -> p g c u", u=2),
+            )
+
+        def quantise_e(i, k0, k1):
+            if k0 == 0:
+                live["codes", i] = work.tile([P, N // 4], U32, name="codes", align_bytes=64)
+                live["scales", i] = work.tile([P, N // 4], U8, name="scales", align_bytes=64)
+            nc.vector.quantize_mx(
+                out=live["codes", i][:, k0 // 4 : k1 // 4].bitcast(FP8X4),
+                scales=live["scales", i][:, k0 // 4 : k1 // 4],
+                in_=live["grouped", i][:, k0:k1],
+            )
+
+        def reciprocals(i0, i1):
+            nc.vector.reciprocal(out=rinvs[:, i0:i1], in_=rowsums[:, i0:i1])
+
+        def weighted_sum(i, g0, g1):
+            if g0 == 0:
+                live["acc", i] = ps_o.tile([P, D], F32, name="acc")
+            for g in range(g0, g1):
+                cols = slice(g * P, (g + 1) * P)
+                nc.tensor.matmul_mx(
+                    out=live["acc", i][:],
+                    lhsT=live["codes", i][:, cols].bitcast(FP8X4),
+                    lhsT_scale=live["scales", i][:, cols],
+                    rhs=v_codes[:, cols].bitcast(FP8X4),
+                    rhs_scale=v_scales[:, cols],
+                    start=(g == 0),
+                    stop=(g == 7),
+                )
+
+        def normalise(i):
+            o_sb = small.tile([P, D], F32, name="o_sb")
+            nc.scalar.activation(out=o_sb[:], in_=live["acc", i][:], func=ACT.Copy, scale=rinvs[:, i : i + 1])
+            nc.sync.dma_start(out=out[i * P : (i + 1) * P, :], in_=o_sb[:])
+
+        def has(i):
+            return 0 <= i < NT
+
+        def vector_drains(i, c):
+            return c == 0 and i % 3 == 0
+
+        v_copy = nc.vector.tensor_copy
+        s_copy = nc.scalar.copy
+
+        flip_q(0, 1)
+        for g in range(3):
+            flip_k(g)
+        regroup(v_grouped, v_raw[:].rearrange("p g x -> p (g x)"))
+        for n in range(NT):
+            if has(n - 4):
+                normalise(n - 4)
+            for b in range(NB):
+                if has(n - 2) and 1 <= b <= 3:
+                    flip_e(n - 2, b - 1)
+                    if not vector_drains(n - 2, b - 1):
+                        drain_e(n - 2, b - 1, s_copy)
+                scores(n, b)
+                if n == 0 and b + 3 < NB:
+                    flip_k(b + 3)
+                if n == 0 and b == 5:
+                    flip_q(*Q_REST[0])
+                if b == 0 and has(n - 1):
+                    row_bias(n - 1)
+                    exponentials(n - 1, 0, N, rowsums[:, n - 1 : n])
+                    if has(n - 3) and n % 2 == 1:
+                        reciprocals(n - 3, n - 1)
+                if n == 1 and 1 <= b <= 3:
+                    flip_q(*Q_REST[b])
+                if b == 2 and has(n - 3):
+                    quantise_e(n - 3, 0, N)
+                if b == 4 and has(n - 2) and vector_drains(n - 2, 0):
+                    drain_e(n - 2, 0, v_copy)
+            if n == 2:
+                nc.vector.quantize_mx(out=v_codes[:].bitcast(FP8X4), scales=v_scales[:], in_=v_grouped[:])
+            if has(n - 3):
+                weighted_sum(n - 3, 0, 8)
+            if has(n - 2):
+                flip_e(n - 2, 3)
+                drain_e(n - 2, 3, s_copy)
+
+        a, y, z = NT - 3, NT - 2, NT - 1
+        row_bias(z)
+        normalise(NT - 4)
+        last = small.tile([P, 4], F32, name="last")
+        for c in range(3):
+            flip_e(y, c)
+        exponentials(z, 0, 1024, last[:, 0:1])
+        drain_e(y, 0, v_copy)
+        quantise_e(a, 0, N)
+        reciprocals(y, y + 1)
+        exponentials(z, 1024, 2048, last[:, 1:2])
+        drain_e(y, 1, v_copy)
+        flip_e(y, 3)
+        weighted_sum(a, 0, 8)
+        drain_e(y, 2, v_copy)
+        exponentials(z, 2048, 3072, last[:, 2:3])
+        normalise(a)
+        drain_e(y, 3, v_copy)
+        flip_e(z, 0)
+        flip_e(z, 1)
+        exponentials(z, 3072, 4096, last[:, 3:4])
+        quantise_e(y, 0, N)
+        drain_e(z, 0, s_copy)
+        flip_e(z, 2)
+        weighted_sum(y, 0, 8)
+        drain_e(z, 1, s_copy)
+        flip_e(z, 3)
+        quantise_e(z, 0, 1024)
+        drain_e(z, 2, s_copy)
+        drain_e(z, 3, v_copy)
+        normalise(y)
+        nc.vector.tensor_reduce(out=rowsums[:, z : z + 1], in_=last[:], axis=mybir.AxisListType.X, op=ALU.add)
+        quantise_e(z, 1024, 2048)
+        reciprocals(z, z + 1)
+        weighted_sum(z, 0, 4)
+        quantise_e(z, 2048, 3072)
+        quantise_e(z, 3072, 4096)
+        weighted_sum(z, 4, 8)
+        normalise(z)

@@ -265,14 +265,17 @@ def tile_scaled_dot_product_kernel(tc, q, k, v, out):
             flip_k(g)
         regroup(v_grouped, v_raw[:].rearrange("p g x -> p (g x)"))
         for n in range(NT):
-            if has(n - 4):
-                normalise(n - 4)
             for b in range(NB):
                 if has(n - 2) and 1 <= b <= 3:
                     flip_e(n - 2, b - 1)
                     if not vector_drains(n - 2, b - 1):
                         drain_e(n - 2, b - 1, s_copy)
                 scores(n, b)
+                if b == 0 and has(n - 3):
+                    flip_e(n - 3, 3)
+                    drain_e(n - 3, 3, s_copy)
+                    if has(n - 4):
+                        normalise(n - 4)
                 if n == 0 and b + 3 < NB:
                     flip_k(b + 3)
                 if n == 0 and b == 5:
@@ -284,7 +287,7 @@ def tile_scaled_dot_product_kernel(tc, q, k, v, out):
                         reciprocals(n - 3, n - 1)
                 if n == 1 and 1 <= b <= 3:
                     flip_q(*Q_REST[b])
-                if b == 2 and has(n - 3):
+                if b == 3 and has(n - 3):
                     quantise_e(n - 3, 0, N)
                 if b == 4 and has(n - 2) and vector_drains(n - 2, 0):
                     drain_e(n - 2, 0, v_copy)
@@ -292,11 +295,10 @@ def tile_scaled_dot_product_kernel(tc, q, k, v, out):
                 nc.vector.quantize_mx(out=v_codes[:].bitcast(FP8X4), scales=v_scales[:], in_=v_grouped[:])
             if has(n - 3):
                 weighted_sum(n - 3, 0, 8)
-            if has(n - 2):
-                flip_e(n - 2, 3)
-                drain_e(n - 2, 3, s_copy)
 
         a, y, z = NT - 3, NT - 2, NT - 1
+        flip_e(a, 3)
+        drain_e(a, 3, s_copy)
         row_bias(z)
         normalise(NT - 4)
         last = small.tile([P, 4], F32, name="last")

@@ -266,30 +266,32 @@ def tile_scaled_dot_product_kernel(tc, q, k, v, out):
         regroup(v_grouped, v_raw[:].rearrange("p g x -> p (g x)"))
         for n in range(NT):
             for b in range(NB):
-                if has(n - 2) and 1 <= b <= 3:
-                    flip_e(n - 2, b - 1)
-                    if not vector_drains(n - 2, b - 1):
-                        drain_e(n - 2, b - 1, s_copy)
+                if has(n - 2) and 3 <= b <= 5:
+                    flip_e(n - 2, b - 3)
+                    if not vector_drains(n - 2, b - 3):
+                        drain_e(n - 2, b - 3, s_copy)
                 scores(n, b)
-                if b == 0 and has(n - 3):
-                    flip_e(n - 3, 3)
-                    drain_e(n - 3, 3, s_copy)
-                    if has(n - 4):
-                        normalise(n - 4)
                 if n == 0 and b + 3 < NB:
                     flip_k(b + 3)
                 if n == 0 and b == 5:
                     flip_q(*Q_REST[0])
                 if b == 0 and has(n - 1):
                     row_bias(n - 1)
-                    exponentials(n - 1, 0, N, rowsums[:, n - 1 : n])
                     if has(n - 3) and n % 2 == 1:
                         reciprocals(n - 3, n - 1)
+                if b == 2:
+                    if has(n - 3):
+                        flip_e(n - 3, 3)
+                        drain_e(n - 3, 3, s_copy)
+                    if has(n - 4):
+                        normalise(n - 4)
+                    if has(n - 1):
+                        exponentials(n - 1, 0, N, rowsums[:, n - 1 : n])
                 if n == 1 and 1 <= b <= 3:
                     flip_q(*Q_REST[b])
-                if b == 3 and has(n - 3):
+                if b == 4 and has(n - 3):
                     quantise_e(n - 3, 0, N)
-                if b == 4 and has(n - 2) and vector_drains(n - 2, 0):
+                if b == 6 and has(n - 2) and vector_drains(n - 2, 0):
                     drain_e(n - 2, 0, v_copy)
             if n == 2:
                 nc.vector.quantize_mx(out=v_codes[:].bitcast(FP8X4), scales=v_scales[:], in_=v_grouped[:])

@@ -22,8 +22,6 @@ FLOPS = 2 * N * N * (D + D)
 
 ROOT = math.sqrt(128.0)
 SCALE = 1.0 / ROOT
-ROOT_PIECES = (11.3125, 0.0012054443359375, 3.0547380447387695e-06)
-assert abs(sum(ROOT_PIECES) - ROOT) < 1e-10
 Q_REST = ((1, 8), (8, 16), (16, 24), (24, 32))
 
 
@@ -67,22 +65,23 @@ def tile_scaled_dot_product_kernel(tc, q, k, v, out):
             compare_op=ALU.is_ge,
             fill=1.0,
             base=0,
-            pattern=[[-1, P]],
-            channel_multiplier=1,
+            pattern=[[1, P]],
+            channel_multiplier=-1,
         )
         ident_f = const.tile([P, P], F32)
         make_identity(nc, ident_f[:])
-        tri = []
-        for i in range(3):
-            m_i = const.tile([P, P], BF16, name="tri%d" % i)
-            nc.vector.tensor_scalar(
-                out=m_i[:].rearrange("q (u p b) -> q u p b", u=2, b=2),
-                in0=upper[:].rearrange("q (p u b) -> q u p b", u=2, b=2),
-                scalar1=ROOT_PIECES[i],
-                scalar2=None,
-                op0=ALU.mult,
-            )
-            tri.append(m_i)
+        ones = const.tile([P, P], F32)
+        nc.vector.memset(ones[:], 1.0)
+        added = []
+        for i, source in enumerate((upper, ones)):
+            a_i = const.tile([P, P], F32, name="added%d" % i)
+            nc.vector.tensor_scalar(out=a_i[:], in0=source[:], scalar1=ROOT, scalar2=None, op0=ALU.mult)
+            added.append(a_i)
+        shuffle = const.tile([P, P], F32)
+        nc.vector.tensor_copy(
+            out=shuffle[:].rearrange("q (u p b) -> q u p b", u=2, b=2),
+            in_=ident_f[:].rearrange("q (p u b) -> q u p b", u=2, b=2),
+        )
 
         qT = const.tile([P, N], BF16)
         kT = const.tile([P, N], BF16)
@@ -128,57 +127,36 @@ def tile_scaled_dot_product_kernel(tc, q, k, v, out):
             lq = qT[:, i * P : (i + 1) * P]
             if b == 0:
                 live["stash", i] = stash_pool.tile([P, N], F32, name="stash")
-                live["mparts", i] = small.tile([P, 16], F32, name="mparts")
-                live["n", i] = 0
+                live["mparts", i] = small.tile([P, NB], F32, name="mparts")
             bank = ps_s.tile([P, BANK], F32, name="s_ps")
             s_ps = bank[:].rearrange("q (u x) -> q u x", u=2)
-            keys = kT[:, k0 : k0 + BANK].rearrange("d (u x) -> d u x", u=2)
-            stash = live["stash", i][:, k0 : k0 + BANK].rearrange("q (u x) -> q u x", u=2)
-            lo, hi = 64 * sd, 64 * sd + 64
-            if b != bd:
-                nc.tensor.matmul(out=bank[:], lhsT=lq, rhs=kT[:, k0 : k0 + BANK], start=True, stop=True)
-            else:
-                if sd > 0:
-                    nc.tensor.matmul(out=s_ps[:, :, 0:lo], lhsT=lq, rhs=keys[:, :, 0:lo], start=True, stop=True)
-                nc.tensor.matmul(out=s_ps[:, :, lo:hi], lhsT=lq, rhs=keys[:, :, lo:hi], start=True, stop=False)
-                for j in range(3):
+            nc.tensor.matmul(out=bank[:], lhsT=lq, rhs=kT[:, k0 : k0 + BANK], start=True, stop=(b != bd))
+            if b == bd:
+                for j in range(sd, 4):
                     nc.tensor.matmul(
-                        out=s_ps[:, :, lo:hi],
-                        lhsT=ident[:],
-                        rhs=tri[j][:].rearrange("q (u x) -> q u x", u=2),
+                        out=s_ps[:, :, 64 * j : 64 * j + 64],
+                        lhsT=added[0 if j == sd else 1][:],
+                        rhs=shuffle[:].rearrange("q (u x) -> q u x", u=2),
                         start=False,
-                        stop=(j == 2),
+                        stop=(j == 3),
+                        is_transpose=True,
                     )
-                if sd < 3:
-                    nc.tensor.matmul(out=s_ps[:, :, hi:256], lhsT=lq, rhs=keys[:, :, hi:256], start=True, stop=True)
-            if b < bd:
-                parts = [(0, 256, 0.0)]
-            elif b > bd:
-                parts = [(0, 256, ROOT)]
-            else:
-                parts = [(0, hi, 0.0)]
-                if sd < 3:
-                    parts.append((hi, 256, ROOT))
-            for c0, c1, shift in parts:
-                n_parts = live["n", i]
-                nc.vector.tensor_scalar(
-                    out=stash[:, :, c0:c1],
-                    in0=s_ps[:, :, c0:c1],
-                    scalar1=shift,
-                    scalar2=None,
-                    op0=ALU.add,
-                    op1=ALU.max,
-                    accum_out=live["mparts", i][:, n_parts : n_parts + 1],
-                )
-                live["n", i] = n_parts + 1
+            nc.vector.tensor_scalar(
+                out=live["stash", i][:, k0 : k0 + BANK],
+                in0=bank[:],
+                scalar1=ROOT if b > bd else 0.0,
+                scalar2=None,
+                op0=ALU.add,
+                op1=ALU.max,
+                accum_out=live["mparts", i][:, b : b + 1],
+            )
 
         def row_bias(i):
-            n_parts = live["n", i]
-            junk = small.tile([P, 16], F32, name="junk")
+            junk = small.tile([P, NB], F32, name="junk")
             nbias = small.tile([P, 1], F32, name="nbias")
             nc.vector.tensor_scalar(
-                out=junk[:, 0:n_parts],
-                in0=live["mparts", i][:, 0:n_parts],
+                out=junk[:],
+                in0=live["mparts", i][:],
                 scalar1=-SCALE,
                 scalar2=None,
                 op0=ALU.mult,
@@ -255,7 +233,7 @@ def tile_scaled_dot_product_kernel(tc, q, k, v, out):
             return 0 <= i < NT
 
         def vector_drains(i, c):
-            return c == 0 and i % 3 == 0
+            return i == NT - 3 or (c == 0 and i % 3 == 0)
 
         v_copy = nc.vector.tensor_copy
         s_copy = nc.scalar.copy
@@ -291,7 +269,7 @@ def tile_scaled_dot_product_kernel(tc, q, k, v, out):
                     flip_q(*Q_REST[b])
                 if b == 4 and has(n - 3):
                     quantise_e(n - 3, 0, N)
-                if b == 6 and has(n - 2) and vector_drains(n - 2, 0):
+                if b == 6 and has(n - 2) and n < NT - 1 and vector_drains(n - 2, 0):
                     drain_e(n - 2, 0, v_copy)
             if n == 2:
                 nc.vector.quantize_mx(out=v_codes[:].bitcast(FP8X4), scales=v_scales[:], in_=v_grouped[:])
@@ -299,41 +277,45 @@ def tile_scaled_dot_product_kernel(tc, q, k, v, out):
                 weighted_sum(n - 3, 0, 8)
 
         a, y, z = NT - 3, NT - 2, NT - 1
-        flip_e(a, 3)
-        drain_e(a, 3, s_copy)
+        drain_e(a, 0, s_copy)
         row_bias(z)
         normalise(NT - 4)
         last = small.tile([P, 4], F32, name="last")
-        for c in range(3):
-            flip_e(y, c)
         exponentials(z, 0, 1024, last[:, 0:1])
+        drain_e(a, 1, v_copy)
+        flip_e(a, 3)
+        drain_e(a, 2, v_copy)
+        flip_e(y, 0)
+        drain_e(a, 3, v_copy)
+        flip_e(y, 1)
+        flip_e(y, 2)
+        exponentials(z, 1024, 2048, last[:, 1:2])
         drain_e(y, 0, v_copy)
         quantise_e(a, 0, N)
-        reciprocals(y, y + 1)
-        exponentials(z, 1024, 2048, last[:, 1:2])
-        drain_e(y, 1, v_copy)
         flip_e(y, 3)
+        reciprocals(y, y + 1)
+        drain_e(y, 1, v_copy)
         weighted_sum(a, 0, 8)
-        drain_e(y, 2, v_copy)
-        exponentials(z, 2048, 3072, last[:, 2:3])
-        normalise(a)
-        drain_e(y, 3, v_copy)
         flip_e(z, 0)
+        exponentials(z, 2048, 3072, last[:, 2:3])
+        drain_e(y, 2, v_copy)
         flip_e(z, 1)
+        drain_e(y, 3, v_copy)
         exponentials(z, 3072, 4096, last[:, 3:4])
-        quantise_e(y, 0, N)
+        normalise(a)
         drain_e(z, 0, s_copy)
         flip_e(z, 2)
-        weighted_sum(y, 0, 8)
+        quantise_e(y, 0, N)
         drain_e(z, 1, s_copy)
         flip_e(z, 3)
+        weighted_sum(y, 0, 8)
         quantise_e(z, 0, 1024)
         drain_e(z, 2, s_copy)
-        drain_e(z, 3, v_copy)
-        normalise(y)
         nc.vector.tensor_reduce(out=rowsums[:, z : z + 1], in_=last[:], axis=mybir.AxisListType.X, op=ALU.add)
         quantise_e(z, 1024, 2048)
         reciprocals(z, z + 1)
+        drain_e(z, 3, s_copy)
+        normalise(y)
         weighted_sum(z, 0, 4)
         quantise_e(z, 2048, 3072)
         quantise_e(z, 3072, 4096)

@@ -92,15 +92,14 @@ def tile_scaled_dot_product_kernel(tc, q, k, v, out):
         rinvs = const.tile([P, NT], F32)
 
         def regroup(dst, src):
-            for h in range(2):
-                nc.gpsimd.tensor_scalar(
-                    out=dst[:, 2048 * h : 2048 * h + 2048].rearrange("p (g c t) -> p g c t", g=4, t=4),
-                    in0=src[:, 2048 * h : 2048 * h + 2048].rearrange("p (g t c) -> p g c t", g=4, t=4),
-                    scalar1=1.0,
-                    scalar2=0.0,
-                    op0=ALU.mult,
-                    op1=ALU.add,
-                )
+            nc.gpsimd.tensor_scalar(
+                out=dst.rearrange("p (g c t) -> p g c t", g=2, t=4),
+                in0=src.rearrange("p (g t c) -> p g c t", g=2, t=4),
+                scalar1=1.0,
+                scalar2=0.0,
+                op0=ALU.mult,
+                op1=ALU.add,
+            )
 
         def flip_q(j0, j1):
             tp = ps_t.tile([P, 8, P], BF16, name="tp_q", tag="tp")
@@ -152,16 +151,11 @@ def tile_scaled_dot_product_kernel(tc, q, k, v, out):
             )
 
         def row_bias(i):
-            junk = small.tile([P, NB], F32, name="junk")
+            top = small.tile([P, 1], F32, name="top")
             nbias = small.tile([P, 1], F32, name="nbias")
-            nc.vector.tensor_scalar(
-                out=junk[:],
-                in0=live["mparts", i][:],
-                scalar1=-SCALE,
-                scalar2=None,
-                op0=ALU.mult,
-                op1=ALU.min,
-                accum_out=nbias[:, 0:1],
+            nc.vector.tensor_reduce(out=top[:], in_=live["mparts", i][:], axis=mybir.AxisListType.X, op=ALU.max)
+            nc.gpsimd.tensor_scalar(
+                out=nbias[:], in0=top[:], scalar1=-SCALE, scalar2=0.0, op0=ALU.mult, op1=ALU.add
             )
             live["nbias", i] = nbias
 
@@ -233,7 +227,7 @@ def tile_scaled_dot_product_kernel(tc, q, k, v, out):
             return 0 <= i < NT
 
         def vector_drains(i, c):
-            return i == NT - 3 or (c == 0 and i % 3 == 0)
+            return i == NT - 3 or (c == 0 and i % 2 == 0)
 
         v_copy = nc.vector.tensor_copy
         s_copy = nc.scalar.copy
@@ -241,13 +235,12 @@ def tile_scaled_dot_product_kernel(tc, q, k, v, out):
         flip_q(0, 1)
         for g in range(3):
             flip_k(g)
-        regroup(v_grouped, v_raw[:].rearrange("p g x -> p (g x)"))
         for n in range(NT):
             for b in range(NB):
-                if has(n - 2) and 3 <= b <= 5:
-                    flip_e(n - 2, b - 3)
-                    if not vector_drains(n - 2, b - 3):
-                        drain_e(n - 2, b - 3, s_copy)
+                if has(n - 2) and 4 <= b <= 6:
+                    flip_e(n - 2, b - 4)
+                    if not vector_drains(n - 2, b - 4):
+                        drain_e(n - 2, b - 4, s_copy)
                 scores(n, b)
                 if n == 0 and b + 3 < NB:
                     flip_k(b + 3)
@@ -257,7 +250,9 @@ def tile_scaled_dot_product_kernel(tc, q, k, v, out):
                     row_bias(n - 1)
                     if has(n - 3) and n % 2 == 1:
                         reciprocals(n - 3, n - 1)
-                if b == 2:
+                if b == 0 and has(n - 4):
+                    weighted_sum(n - 4, 0, 8)
+                if b == 3:
                     if has(n - 3):
                         flip_e(n - 3, 3)
                         drain_e(n - 3, 3, s_copy)
@@ -265,20 +260,22 @@ def tile_scaled_dot_product_kernel(tc, q, k, v, out):
                         normalise(n - 4)
                     if has(n - 1):
                         exponentials(n - 1, 0, N, rowsums[:, n - 1 : n])
+                if 1 <= n <= 2 and 1 <= b <= 2:
+                    part = slice(1024 * (2 * n + b - 3), 1024 * (2 * n + b - 2))
+                    regroup(v_grouped[:, part], v_raw[:].rearrange("p g x -> p (g x)")[:, part])
                 if n == 1 and 1 <= b <= 3:
                     flip_q(*Q_REST[b])
                 if b == 4 and has(n - 3):
                     quantise_e(n - 3, 0, N)
-                if b == 6 and has(n - 2) and n < NT - 1 and vector_drains(n - 2, 0):
+                if b == 7 and has(n - 2) and n < NT - 1 and vector_drains(n - 2, 0):
                     drain_e(n - 2, 0, v_copy)
             if n == 2:
                 nc.vector.quantize_mx(out=v_codes[:].bitcast(FP8X4), scales=v_scales[:], in_=v_grouped[:])
-            if has(n - 3):
-                weighted_sum(n - 3, 0, 8)
 
         a, y, z = NT - 3, NT - 2, NT - 1
         drain_e(a, 0, s_copy)
         row_bias(z)
+        weighted_sum(NT - 4, 0, 8)
         normalise(NT - 4)
         last = small.tile([P, 4], F32, name="last")
         exponentials(z, 0, 1024, last[:, 0:1])

@@ -52,6 +52,8 @@ def tile_scaled_dot_product_kernel(tc, q, k, v, out):
             nc.sync.dma_start(out=q_raw[:, j0:j1, :], in_=q_view[:, j0:j1, :])
         nc.sync.dma_start(out=v_raw[:], in_=v_view)
 
+        blank = const.tile([P, BANK], BF16)
+        nc.vector.memset(blank[:], 0.0)
         warm = const.tile([P, 2], F32)
         nc.vector.memset(warm[:, 0:1], 0.0)
         nc.scalar.activation(out=warm[:, 1:2], in_=warm[:, 0:1], func=ACT.Exp)
@@ -232,6 +234,9 @@ def tile_scaled_dot_product_kernel(tc, q, k, v, out):
         v_copy = nc.vector.tensor_copy
         s_copy = nc.scalar.copy
 
+        for j in range(5):
+            idle = ps_s.tile([P, BANK], F32, name="s_ps")
+            nc.tensor.matmul(out=idle[:], lhsT=blank[:, 0:P], rhs=blank[:], start=True, stop=True)
         flip_q(0, 1)
         for g in range(3):
             flip_k(g)

@@ -34,8 +34,8 @@ def tile_scaled_dot_product_kernel(tc, q, k, v, out):
         grouped_pool = ctx.enter_context(tc.tile_pool(name="grouped", bufs=3))
         work = ctx.enter_context(tc.tile_pool(name="work", bufs=2))
         small = ctx.enter_context(tc.tile_pool(name="small", bufs=6))
-        ps_s = ctx.enter_context(tc.psum_pool(name="ps_s", bufs=4))
-        ps_t = ctx.enter_context(tc.psum_pool(name="ps_t", bufs=3))
+        ps_s = ctx.enter_context(tc.psum_pool(name="ps_s", bufs=3))
+        ps_t = ctx.enter_context(tc.psum_pool(name="ps_t", bufs=4))
         ps_o = ctx.enter_context(tc.psum_pool(name="ps_o", bufs=1))
         ctx.enter_context(tc.manual_schedule())
 
@@ -46,7 +46,7 @@ def tile_scaled_dot_product_kernel(tc, q, k, v, out):
         k_view = k.rearrange("(g p t) d -> p g (t d)", p=P, t=4)
         v_view = v.rearrange("(g p t) d -> p g (t d)", p=P, t=4)
         nc.sync.dma_start(out=q_raw[:, 0:1, :], in_=q_view[:, 0:1, :])
-        for g in range(NB):
+        for g in list(range(1, NB)) + [0]:
             nc.sync.dma_start(out=k_raw[:, g : g + 1, :], in_=k_view[:, g : g + 1, :])
         for j0, j1 in Q_REST:
             nc.sync.dma_start(out=q_raw[:, j0:j1, :], in_=q_view[:, j0:j1, :])
@@ -126,7 +126,7 @@ def tile_scaled_dot_product_kernel(tc, q, k, v, out):
             bd, sd = i // 4, i % 4
             k0 = b * BANK
             lq = qT[:, i * P : (i + 1) * P]
-            if b == 0:
+            if ("stash", i) not in live:
                 live["stash", i] = stash_pool.tile([P, N], F32, name="stash")
                 live["mparts", i] = small.tile([P, NB], F32, name="mparts")
             bank = ps_s.tile([P, BANK], F32, name="s_ps")
@@ -229,47 +229,42 @@ def tile_scaled_dot_product_kernel(tc, q, k, v, out):
             return 0 <= i < NT
 
         def vector_drains(i, c):
-            return i == NT - 3 or (c == 0 and i % 2 == 0)
+            return i == NT - 3 or (c == 0 and i % 5 in (0, 2))
 
         v_copy = nc.vector.tensor_copy
         s_copy = nc.scalar.copy
 
-        for j in range(5):
+        for j in range(3):
             idle = ps_s.tile([P, BANK], F32, name="s_ps")
             nc.tensor.matmul(out=idle[:], lhsT=blank[:, 0:P], rhs=blank[:], start=True, stop=True)
         flip_q(0, 1)
-        for g in range(3):
+        for g in range(1, 4):
             flip_k(g)
         for n in range(NT):
             for b in range(NB):
-                if has(n - 2) and 4 <= b <= 6:
-                    flip_e(n - 2, b - 4)
-                    if not vector_drains(n - 2, b - 4):
-                        drain_e(n - 2, b - 4, s_copy)
-                scores(n, b)
+                scores(n, (b + 1) % NB if n == 0 else b)
                 if n == 0 and b + 3 < NB:
-                    flip_k(b + 3)
+                    flip_k((b + 4) % NB)
                 if n == 0 and b == 5:
                     flip_q(*Q_REST[0])
                 if b == 0 and has(n - 1):
                     row_bias(n - 1)
                     if has(n - 3) and n % 2 == 1:
                         reciprocals(n - 3, n - 1)
-                if b == 0 and has(n - 4):
-                    weighted_sum(n - 4, 0, 8)
-                if b == 3:
-                    if has(n - 3):
-                        flip_e(n - 3, 3)
-                        drain_e(n - 3, 3, s_copy)
-                    if has(n - 4):
-                        normalise(n - 4)
-                    if has(n - 1):
-                        exponentials(n - 1, 0, N, rowsums[:, n - 1 : n])
+                if b == 0 and has(n - 1):
+                    exponentials(n - 1, 0, N, rowsums[:, n - 1 : n - 1 + 1])
                 if 1 <= n <= 2 and 1 <= b <= 2:
                     part = slice(1024 * (2 * n + b - 3), 1024 * (2 * n + b - 2))
                     regroup(v_grouped[:, part], v_raw[:].rearrange("p g x -> p (g x)")[:, part])
                 if n == 1 and 1 <= b <= 3:
                     flip_q(*Q_REST[b])
+                if b == 7 and has(n - 3):
+                    weighted_sum(n - 3, 0, 8)
+                    normalise(n - 3)
+                if has(n - 2) and 2 <= b <= 5:
+                    flip_e(n - 2, b - 2)
+                    if not vector_drains(n - 2, b - 2):
+                        drain_e(n - 2, b - 2, s_copy)
                 if b == 4 and has(n - 3):
                     quantise_e(n - 3, 0, N)
                 if b == 7 and has(n - 2) and n < NT - 1 and vector_drains(n - 2, 0):
@@ -278,48 +273,44 @@ def tile_scaled_dot_product_kernel(tc, q, k, v, out):
                 nc.vector.quantize_mx(out=v_codes[:].bitcast(FP8X4), scales=v_scales[:], in_=v_grouped[:])
 
         a, y, z = NT - 3, NT - 2, NT - 1
-        drain_e(a, 0, s_copy)
-        row_bias(z)
-        weighted_sum(NT - 4, 0, 8)
-        normalise(NT - 4)
         last = small.tile([P, 4], F32, name="last")
-        exponentials(z, 0, 1024, last[:, 0:1])
+        drain_e(a, 0, s_copy)
         drain_e(a, 1, v_copy)
-        flip_e(a, 3)
+        row_bias(z)
+        exponentials(z, 0, 1024, last[:, 0:1])
         drain_e(a, 2, v_copy)
         flip_e(y, 0)
         drain_e(a, 3, v_copy)
         flip_e(y, 1)
         flip_e(y, 2)
+        flip_e(y, 3)
         exponentials(z, 1024, 2048, last[:, 1:2])
         drain_e(y, 0, v_copy)
-        quantise_e(a, 0, N)
-        flip_e(y, 3)
-        reciprocals(y, y + 1)
         drain_e(y, 1, v_copy)
-        weighted_sum(a, 0, 8)
         flip_e(z, 0)
-        exponentials(z, 2048, 3072, last[:, 2:3])
-        drain_e(y, 2, v_copy)
         flip_e(z, 1)
+        quantise_e(a, 0, N)
+        exponentials(z, 2048, 3072, last[:, 2:3])
+        drain_e(z, 0, s_copy)
+        reciprocals(y, y + 1)
+        drain_e(y, 2, v_copy)
+        weighted_sum(a, 0, 8)
+        flip_e(z, 2)
         drain_e(y, 3, v_copy)
         exponentials(z, 3072, 4096, last[:, 3:4])
-        normalise(a)
-        drain_e(z, 0, s_copy)
-        flip_e(z, 2)
-        quantise_e(y, 0, N)
         drain_e(z, 1, s_copy)
+        normalise(a)
+        quantise_e(y, 0, N)
         flip_e(z, 3)
-        weighted_sum(y, 0, 8)
-        quantise_e(z, 0, 1024)
         drain_e(z, 2, s_copy)
-        nc.vector.tensor_reduce(out=rowsums[:, z : z + 1], in_=last[:], axis=mybir.AxisListType.X, op=ALU.add)
-        quantise_e(z, 1024, 2048)
-        reciprocals(z, z + 1)
+        quantise_e(z, 0, 2048)
+        weighted_sum(y, 0, 8)
         drain_e(z, 3, s_copy)
+        nc.vector.tensor_reduce(out=rowsums[:, z : z + 1], in_=last[:], axis=mybir.AxisListType.X, op=ALU.add)
+        quantise_e(z, 2048, 3072)
+        reciprocals(z, z + 1)
         normalise(y)
         weighted_sum(z, 0, 4)
-        quantise_e(z, 2048, 3072)
         quantise_e(z, 3072, 4096)
         weighted_sum(z, 4, 8)
         normalise(z)

@@ -34,9 +34,8 @@ def tile_scaled_dot_product_kernel(tc, q, k, v, out):
         grouped_pool = ctx.enter_context(tc.tile_pool(name="grouped", bufs=3))
         work = ctx.enter_context(tc.tile_pool(name="work", bufs=2))
         small = ctx.enter_context(tc.tile_pool(name="small", bufs=6))
-        ps_s = ctx.enter_context(tc.psum_pool(name="ps_s", bufs=3))
+        ps_s = ctx.enter_context(tc.psum_pool(name="ps_s", bufs=4))
         ps_t = ctx.enter_context(tc.psum_pool(name="ps_t", bufs=4))
-        ps_o = ctx.enter_context(tc.psum_pool(name="ps_o", bufs=1))
         ctx.enter_context(tc.manual_schedule())
 
         q_raw = const.tile([P, NT, D], BF16)
@@ -129,7 +128,7 @@ def tile_scaled_dot_product_kernel(tc, q, k, v, out):
             if ("stash", i) not in live:
                 live["stash", i] = stash_pool.tile([P, N], F32, name="stash")
                 live["mparts", i] = small.tile([P, NB], F32, name="mparts")
-            bank = ps_s.tile([P, BANK], F32, name="s_ps")
+            bank = ps_s.tile([P, BANK], F32, name="s_ps", tag="s_ps")
             s_ps = bank[:].rearrange("q (u x) -> q u x", u=2)
             nc.tensor.matmul(out=bank[:], lhsT=lq, rhs=kT[:, k0 : k0 + BANK], start=True, stop=(b != bd))
             if b == bd:
@@ -207,7 +206,7 @@ def tile_scaled_dot_product_kernel(tc, q, k, v, out):
 
         def weighted_sum(i, g0, g1):
             if g0 == 0:
-                live["acc", i] = ps_o.tile([P, D], F32, name="acc")
+                live["acc", i] = ps_s.tile([P, D], F32, name="acc", tag="s_ps")
             for g in range(g0, g1):
                 cols = slice(g * P, (g + 1) * P)
                 nc.tensor.matmul_mx(
@@ -222,14 +221,16 @@ def tile_scaled_dot_product_kernel(tc, q, k, v, out):
 
         def normalise(i):
             o_sb = small.tile([P, D], F32, name="o_sb")
-            nc.scalar.activation(out=o_sb[:], in_=live["acc", i][:], func=ACT.Copy, scale=rinvs[:, i : i + 1])
+            nc.vector.tensor_tensor(
+                out=o_sb[:], in0=live["acc", i][:], in1=rinvs[:, i : i + 1].to_broadcast([P, D]), op=ALU.mult
+            )
             nc.sync.dma_start(out=out[i * P : (i + 1) * P, :], in_=o_sb[:])
 
         def has(i):
             return 0 <= i < NT
 
         def vector_drains(i, c):
-            return i == NT - 3 or (c == 0 and i % 5 in (0, 2))
+            return i == NT - 3 or (c == 0 and i % 8 == 0)
 
         v_copy = nc.vector.tensor_copy
         s_copy = nc.scalar.copy
@@ -252,20 +253,21 @@ def tile_scaled_dot_product_kernel(tc, q, k, v, out):
                     if has(n - 3) and n % 2 == 1:
                         reciprocals(n - 3, n - 1)
                 if b == 0 and has(n - 1):
-                    exponentials(n - 1, 0, N, rowsums[:, n - 1 : n - 1 + 1])
+                    exponentials(n - 1, 0, N, rowsums[:, n - 1 : n])
                 if 1 <= n <= 2 and 1 <= b <= 2:
                     part = slice(1024 * (2 * n + b - 3), 1024 * (2 * n + b - 2))
                     regroup(v_grouped[:, part], v_raw[:].rearrange("p g x -> p (g x)")[:, part])
                 if n == 1 and 1 <= b <= 3:
                     flip_q(*Q_REST[b])
-                if b == 7 and has(n - 3):
-                    weighted_sum(n - 3, 0, 8)
-                    normalise(n - 3)
-                if has(n - 2) and 2 <= b <= 5:
-                    flip_e(n - 2, b - 2)
-                    if not vector_drains(n - 2, b - 2):
-                        drain_e(n - 2, b - 2, s_copy)
-                if b == 4 and has(n - 3):
+                if b == 1 and has(n - 4):
+                    weighted_sum(n - 4, 0, 8)
+                if b == 1 and has(n - 4):
+                    normalise(n - 4)
+                if has(n - 2) and 3 <= b <= 6:
+                    flip_e(n - 2, b - 3)
+                    if not vector_drains(n - 2, b - 3):
+                        drain_e(n - 2, b - 3, s_copy)
+                if b == 3 and has(n - 3):
                     quantise_e(n - 3, 0, N)
                 if b == 7 and has(n - 2) and n < NT - 1 and vector_drains(n - 2, 0):
                     drain_e(n - 2, 0, v_copy)
@@ -274,9 +276,11 @@ def tile_scaled_dot_product_kernel(tc, q, k, v, out):
 
         a, y, z = NT - 3, NT - 2, NT - 1
         last = small.tile([P, 4], F32, name="last")
+        weighted_sum(a - 1, 0, 8)
         drain_e(a, 0, s_copy)
         drain_e(a, 1, v_copy)
         row_bias(z)
+        normalise(a - 1)
         exponentials(z, 0, 1024, last[:, 0:1])
         drain_e(a, 2, v_copy)
         flip_e(y, 0)

@@ -91,6 +91,8 @@ def tile_scaled_dot_product_kernel(tc, q, k, v, out):
         v_scales = const.tile([P, N // 4], U8, align_bytes=64)
         rowsums = const.tile([P, NT], F32)
         rinvs = const.tile([P, NT], F32)
+        minus_one = const.tile([P, 2], F32)
+        nc.gpsimd.memset(minus_one[:], -1.0)
 
         def regroup(dst, src):
             nc.gpsimd.tensor_scalar(
@@ -152,11 +154,17 @@ def tile_scaled_dot_product_kernel(tc, q, k, v, out):
             )
 
         def row_bias(i):
-            top = small.tile([P, 1], F32, name="top")
+            m = live["mparts", i]
+            top = m[:, 0:1]
+            for j in range(1, 7, 2):
+                higher = small.tile([P, 1], F32, name="top%d" % j)
+                nc.gpsimd.tensor_scalar(
+                    out=higher[:], in0=top, scalar1=m[:, j : j + 1], scalar2=m[:, j + 1 : j + 2], op0=ALU.max, op1=ALU.max
+                )
+                top = higher[:]
             nbias = small.tile([P, 1], F32, name="nbias")
-            nc.vector.tensor_reduce(out=top[:], in_=live["mparts", i][:], axis=mybir.AxisListType.X, op=ALU.max)
             nc.gpsimd.tensor_scalar(
-                out=nbias[:], in0=top[:], scalar1=-SCALE, scalar2=0.0, op0=ALU.mult, op1=ALU.add
+                out=nbias[:], in0=top, scalar1=m[:, 7:8], scalar2=-SCALE, op0=ALU.max, op1=ALU.mult
             )
             live["nbias", i] = nbias
 
@@ -202,7 +210,9 @@ def tile_scaled_dot_product_kernel(tc, q, k, v, out):
             )
 
         def reciprocals(i0, i1):
-            nc.vector.reciprocal(out=rinvs[:, i0:i1], in_=rowsums[:, i0:i1])
+            nc.gpsimd.tensor_tensor(
+                out=rinvs[:, i0:i1], in0=rowsums[:, i0:i1], in1=minus_one[:, 0 : i1 - i0], op=ALU.pow
+            )
 
         def weighted_sum(i, g0, g1):
             if g0 == 0:
@@ -219,10 +229,10 @@ def tile_scaled_dot_product_kernel(tc, q, k, v, out):
                     stop=(g == 7),
                 )
 
-        def normalise(i):
+        def normalise(i, rinv):
             o_sb = small.tile([P, D], F32, name="o_sb")
             nc.vector.tensor_tensor(
-                out=o_sb[:], in0=live["acc", i][:], in1=rinvs[:, i : i + 1].to_broadcast([P, D]), op=ALU.mult
+                out=o_sb[:], in0=live["acc", i][:], in1=rinv.to_broadcast([P, D]), op=ALU.mult
             )
             nc.sync.dma_start(out=out[i * P : (i + 1) * P, :], in_=o_sb[:])
 
@@ -230,7 +240,7 @@ def tile_scaled_dot_product_kernel(tc, q, k, v, out):
             return 0 <= i < NT
 
         def vector_drains(i, c):
-            return i == NT - 3 or (c == 0 and i % 8 == 0)
+            return i == NT - 3 or (c == 0 and i % 4 == 0)
 
         v_copy = nc.vector.tensor_copy
         s_copy = nc.scalar.copy
@@ -248,10 +258,8 @@ def tile_scaled_dot_product_kernel(tc, q, k, v, out):
                     flip_k((b + 4) % NB)
                 if n == 0 and b == 5:
                     flip_q(*Q_REST[0])
-                if b == 0 and has(n - 1):
-                    row_bias(n - 1)
-                    if has(n - 3) and n % 2 == 1:
-                        reciprocals(n - 3, n - 1)
+                if b == 0 and has(n - 3) and n % 2 == 1:
+                    reciprocals(n - 3, n - 1)
                 if b == 0 and has(n - 1):
                     exponentials(n - 1, 0, N, rowsums[:, n - 1 : n])
                 if 1 <= n <= 2 and 1 <= b <= 2:
@@ -262,7 +270,7 @@ def tile_scaled_dot_product_kernel(tc, q, k, v, out):
                 if b == 1 and has(n - 4):
                     weighted_sum(n - 4, 0, 8)
                 if b == 1 and has(n - 4):
-                    normalise(n - 4)
+                    normalise(n - 4, rinvs[:, n - 4 : n - 3])
                 if has(n - 2) and 3 <= b <= 6:
                     flip_e(n - 2, b - 3)
                     if not vector_drains(n - 2, b - 3):
@@ -271,6 +279,7 @@ def tile_scaled_dot_product_kernel(tc, q, k, v, out):
                     quantise_e(n - 3, 0, N)
                 if b == 7 and has(n - 2) and n < NT - 1 and vector_drains(n - 2, 0):
                     drain_e(n - 2, 0, v_copy)
+            row_bias(n)
             if n == 2:
                 nc.vector.quantize_mx(out=v_codes[:].bitcast(FP8X4), scales=v_scales[:], in_=v_grouped[:])
 
@@ -279,8 +288,7 @@ def tile_scaled_dot_product_kernel(tc, q, k, v, out):
         weighted_sum(a - 1, 0, 8)
         drain_e(a, 0, s_copy)
         drain_e(a, 1, v_copy)
-        row_bias(z)
-        normalise(a - 1)
+        normalise(a - 1, rinvs[:, a - 1 : a])
         exponentials(z, 0, 1024, last[:, 0:1])
         drain_e(a, 2, v_copy)
         flip_e(y, 0)
@@ -303,7 +311,7 @@ def tile_scaled_dot_product_kernel(tc, q, k, v, out):
         drain_e(y, 3, v_copy)
         exponentials(z, 3072, 4096, last[:, 3:4])
         drain_e(z, 1, s_copy)
-        normalise(a)
+        normalise(a, rinvs[:, a : a + 1])
         quantise_e(y, 0, N)
         flip_e(z, 3)
         drain_e(z, 2, s_copy)
@@ -312,9 +320,10 @@ def tile_scaled_dot_product_kernel(tc, q, k, v, out):
         drain_e(z, 3, s_copy)
         nc.vector.tensor_reduce(out=rowsums[:, z : z + 1], in_=last[:], axis=mybir.AxisListType.X, op=ALU.add)
         quantise_e(z, 2048, 3072)
-        reciprocals(z, z + 1)
-        normalise(y)
+        rinv = small.tile([P, 1], F32, name="rinv")
+        nc.vector.reciprocal(out=rinv[:], in_=rowsums[:, z : z + 1])
+        normalise(y, rinvs[:, y : y + 1])
         weighted_sum(z, 0, 4)
         quantise_e(z, 3072, 4096)
         weighted_sum(z, 4, 8)
-        normalise(z)
+        normalise(z, rinv[:])

import math
from contextlib import ExitStack

import concourse.mybir as mybir
from concourse.masks import make_identity

F32 = mybir.dt.float32
BF16 = mybir.dt.bfloat16
U32 = mybir.dt.uint32
U8 = mybir.dt.uint8
FP8X4 = mybir.dt.float8_e4m3fn_x4
ALU = mybir.AluOpType
ACT = mybir.ActivationFunctionType

P = 128
N = 4096
D = 128
NT = N // P
BANK = 512
NB = N // BANK
FLOPS = 2 * N * N * (D + D)

ROOT = math.sqrt(128.0)
SCALE = 1.0 / ROOT
Q_REST = ((1, 8), (8, 16), (16, 24), (24, 32))


def tile_scaled_dot_product_kernel(tc, q, k, v, out):
    nc = tc.nc
    with ExitStack() as ctx:
        const = ctx.enter_context(tc.tile_pool(name="const", bufs=1))
        stash_pool = ctx.enter_context(tc.tile_pool(name="stash", bufs=3))
        e_pool = ctx.enter_context(tc.tile_pool(name="e", bufs=3))
        grouped_pool = ctx.enter_context(tc.tile_pool(name="grouped", bufs=3))
        work = ctx.enter_context(tc.tile_pool(name="work", bufs=2))
        small = ctx.enter_context(tc.tile_pool(name="small", bufs=6))
        ps_s = ctx.enter_context(tc.psum_pool(name="ps_s", bufs=4))
        ps_t = ctx.enter_context(tc.psum_pool(name="ps_t", bufs=4))
        ctx.enter_context(tc.manual_schedule())

        q_raw = const.tile([P, NT, D], BF16)
        k_raw = const.tile([P, NB, 4 * D], BF16)
        v_raw = const.tile([P, NB, 4 * D], BF16)
        q_view = q.rearrange("(j p) d -> p j d", p=P)
        k_view = k.rearrange("(g p t) d -> p g (t d)", p=P, t=4)
        v_view = v.rearrange("(g p t) d -> p g (t d)", p=P, t=4)
        nc.sync.dma_start(out=q_raw[:, 0:1, :], in_=q_view[:, 0:1, :])
        for g in list(range(1, NB)) + [0]:
            nc.sync.dma_start(out=k_raw[:, g : g + 1, :], in_=k_view[:, g : g + 1, :])
        for j0, j1 in Q_REST:
            nc.sync.dma_start(out=q_raw[:, j0:j1, :], in_=q_view[:, j0:j1, :])
        nc.sync.dma_start(out=v_raw[:], in_=v_view)

        blank = const.tile([P, BANK], BF16)
        nc.vector.memset(blank[:], 0.0)
        warm = const.tile([P, 2], F32)
        nc.vector.memset(warm[:, 0:1], 0.0)
        nc.scalar.activation(out=warm[:, 1:2], in_=warm[:, 0:1], func=ACT.Exp)
        ident = const.tile([P, P], BF16)
        make_identity(nc, ident[:])
        upper = const.tile([P, P], F32)
        nc.gpsimd.memset(upper[:], 0.0)
        nc.gpsimd.affine_select(
            out=upper[:],
            in_=upper[:],
            compare_op=ALU.is_ge,
            fill=1.0,
            base=0,
            pattern=[[1, P]],
            channel_multiplier=-1,
        )
        ident_f = const.tile([P, P], F32)
        make_identity(nc, ident_f[:])
        ones = const.tile([P, P], F32)
        nc.vector.memset(ones[:], 1.0)
        added = []
        for i, source in enumerate((upper, ones)):
            a_i = const.tile([P, P], F32, name="added%d" % i)
            nc.vector.tensor_scalar(out=a_i[:], in0=source[:], scalar1=ROOT, scalar2=None, op0=ALU.mult)
            added.append(a_i)
        shuffle = const.tile([P, P], F32)
        nc.vector.tensor_copy(
            out=shuffle[:].rearrange("q (u p b) -> q u p b", u=2, b=2),
            in_=ident_f[:].rearrange("q (p u b) -> q u p b", u=2, b=2),
        )

        qT = const.tile([P, N], BF16)
        kT = const.tile([P, N], BF16)
        v_grouped = const.tile([P, N], BF16, align_bytes=64)
        v_codes = const.tile([P, N // 4], U32, align_bytes=64)
        v_scales = const.tile([P, N // 4], U8, align_bytes=64)
        rowsums = const.tile([P, NT], F32)
        rinvs = const.tile([P, NT], F32)
        minus_one = const.tile([P, 2], F32)
        nc.gpsimd.memset(minus_one[:], -1.0)

        def regroup(dst, src):
            nc.gpsimd.tensor_scalar(
                out=dst.rearrange("p (g c t) -> p g c t", g=2, t=4),
                in0=src.rearrange("p (g t c) -> p g c t", g=2, t=4),
                scalar1=1.0,
                scalar2=0.0,
                op0=ALU.mult,
                op1=ALU.add,
            )

        def flip_q(j0, j1):
            tp = ps_t.tile([P, 8, P], BF16, name="tp_q", tag="tp")
            for j in range(j0, j1):
                nc.tensor.transpose(out=tp[:, j - j0, :], in_=q_raw[:, j, :], identity=ident[:])
            nc.scalar.copy(
                out=qT[:, j0 * P : j1 * P], in_=tp[:, 0 : j1 - j0, :].rearrange("p a b -> p (a b)")
            )

        def flip_k(g):
            tp = ps_t.tile([P, 4, P], BF16, name="tp_k", tag="tp")
            for t in range(4):
                nc.tensor.transpose(out=tp[:, t, :], in_=k_raw[:, g, t * P : (t + 1) * P], identity=ident[:])
            nc.scalar.copy(
                out=kT[:, g * BANK : (g + 1) * BANK].rearrange("d (u p b) -> d u p b", u=2, b=2),
                in_=tp[:].rearrange("d (u b) p -> d u p b", u=2),
            )

        live = {}

        def scores(i, b):
            bd, sd = i // 4, i % 4
            k0 = b * BANK
            lq = qT[:, i * P : (i + 1) * P]
            if ("stash", i) not in live:
                live["stash", i] = stash_pool.tile([P, N], F32, name="stash")
                live["mparts", i] = small.tile([P, NB], F32, name="mparts")
            bank = ps_s.tile([P, BANK], F32, name="s_ps", tag="s_ps")
            s_ps = bank[:].rearrange("q (u x) -> q u x", u=2)
            nc.tensor.matmul(out=bank[:], lhsT=lq, rhs=kT[:, k0 : k0 + BANK], start=True, stop=(b != bd))
            if b == bd:
                for j in range(sd, 4):
                    nc.tensor.matmul(
                        out=s_ps[:, :, 64 * j : 64 * j + 64],
                        lhsT=added[0 if j == sd else 1][:],
                        rhs=shuffle[:].rearrange("q (u x) -> q u x", u=2),
                        start=False,
                        stop=(j == 3),
                        is_transpose=True,
                    )
            nc.vector.tensor_scalar(
                out=live["stash", i][:, k0 : k0 + BANK],
                in0=bank[:],
                scalar1=ROOT if b > bd else 0.0,
                scalar2=None,
                op0=ALU.add,
                op1=ALU.max,
                accum_out=live["mparts", i][:, b : b + 1],
            )

        def row_bias(i):
            m = live["mparts", i]
            top = m[:, 0:1]
            for j in range(1, 7, 2):
                higher = small.tile([P, 1], F32, name="top%d" % j)
                nc.gpsimd.tensor_scalar(
                    out=higher[:], in0=top, scalar1=m[:, j : j + 1], scalar2=m[:, j + 1 : j + 2], op0=ALU.max, op1=ALU.max
                )
                top = higher[:]
            nbias = small.tile([P, 1], F32, name="nbias")
            nc.gpsimd.tensor_scalar(
                out=nbias[:], in0=top, scalar1=m[:, 7:8], scalar2=-SCALE, op0=ALU.max, op1=ALU.mult
            )
            live["nbias", i] = nbias

        def exponentials(i, k0, k1, rowsum):
            if k0 == 0:
                live["e", i] = e_pool.tile([P, N], BF16, name="e_sb")
            nc.scalar.activation(
                out=live["e", i][:, k0:k1],
                in_=live["stash", i][:, k0:k1],
                func=ACT.Exp,
                bias=live["nbias", i][:, 0:1],
                scale=SCALE,
                accum_out=rowsum,
            )

        def flip_e(i, c):
            if c == 0:
                live["grouped", i] = grouped_pool.tile([P, N], BF16, name="grouped", align_bytes=64)
            tp = ps_t.tile([P, 4, P], F32, name="tp_e", tag="tp")
            words = live["e", i][:].bitcast(F32)
            for w in range(4):
                nc.tensor.transpose(
                    out=tp[:, w, :], in_=words[:, (4 * c + w) * P : (4 * c + w + 1) * P], identity=ident_f[:]
                )
            live["tp", i, c] = tp

        def drain_e(i, c, copy):
            copy(
                out=live["grouped", i][:]
                .bitcast(F32)[:, 512 * c : 512 * c + 512]
                .rearrange("p (g c u) -> p g c u", g=2, u=2),
                in_=live["tp", i, c][:].rearrange("p (g u) c -> p g c u", u=2),
            )

        def quantise_e(i, k0, k1):
            if k0 == 0:
                live["codes", i] = work.tile([P, N // 4], U32, name="codes", align_bytes=64)
                live["scales", i] = work.tile([P, N // 4], U8, name="scales", align_bytes=64)
            nc.vector.quantize_mx(
                out=live["codes", i][:, k0 // 4 : k1 // 4].bitcast(FP8X4),
                scales=live["scales", i][:, k0 // 4 : k1 // 4],
                in_=live["grouped", i][:, k0:k1],
            )

        def reciprocals(i0, i1):
            nc.gpsimd.tensor_tensor(
                out=rinvs[:, i0:i1], in0=rowsums[:, i0:i1], in1=minus_one[:, 0 : i1 - i0], op=ALU.pow
            )

        def weighted_sum(i, g0, g1):
            if g0 == 0:
                live["acc", i] = ps_s.tile([P, D], F32, name="acc", tag="s_ps")
            for g in range(g0, g1):
                cols = slice(g * P, (g + 1) * P)
                nc.tensor.matmul_mx(
                    out=live["acc", i][:],
                    lhsT=live["codes", i][:, cols].bitcast(FP8X4),
                    lhsT_scale=live["scales", i][:, cols],
                    rhs=v_codes[:, cols].bitcast(FP8X4),
                    rhs_scale=v_scales[:, cols],
                    start=(g == 0),
                    stop=(g == 7),
                )

        def normalise(i, rinv):
            o_sb = small.tile([P, D], F32, name="o_sb")
            nc.vector.tensor_tensor(
                out=o_sb[:], in0=live["acc", i][:], in1=rinv.to_broadcast([P, D]), op=ALU.mult
            )
            nc.sync.dma_start(out=out[i * P : (i + 1) * P, :], in_=o_sb[:])

        def has(i):
            return 0 <= i < NT

        def vector_drains(i, c):
            return i == NT - 3 or (c == 0 and i % 4 == 0)

        v_copy = nc.vector.tensor_copy
        s_copy = nc.scalar.copy

        for j in range(3):
            idle = ps_s.tile([P, BANK], F32, name="s_ps")
            nc.tensor.matmul(out=idle[:], lhsT=blank[:, 0:P], rhs=blank[:], start=True, stop=True)
        flip_q(0, 1)
        for g in range(1, 4):
            flip_k(g)
        for n in range(NT):
            for b in range(NB):
                scores(n, (b + 1) % NB if n == 0 else b)
                if n == 0 and b + 3 < NB:
                    flip_k((b + 4) % NB)
                if n == 0 and b == 5:
                    flip_q(*Q_REST[0])
                if b == 0 and has(n - 3) and n % 2 == 1:
                    reciprocals(n - 3, n - 1)
                if b == 0 and has(n - 1):
                    exponentials(n - 1, 0, N, rowsums[:, n - 1 : n])
                if 1 <= n <= 2 and 1 <= b <= 2:
                    part = slice(1024 * (2 * n + b - 3), 1024 * (2 * n + b - 2))
                    regroup(v_grouped[:, part], v_raw[:].rearrange("p g x -> p (g x)")[:, part])
                if n == 1 and 1 <= b <= 3:
                    flip_q(*Q_REST[b])
                if b == 1 and has(n - 4):
                    weighted_sum(n - 4, 0, 8)
                if b == 1 and has(n - 4):
                    normalise(n - 4, rinvs[:, n - 4 : n - 3])
                if has(n - 2) and 3 <= b <= 6:
                    flip_e(n - 2, b - 3)
                    if not vector_drains(n - 2, b - 3):
                        drain_e(n - 2, b - 3, s_copy)
                if b == 3 and has(n - 3):
                    quantise_e(n - 3, 0, N)
                if b == 7 and has(n - 2) and n < NT - 1 and vector_drains(n - 2, 0):
                    drain_e(n - 2, 0, v_copy)
            row_bias(n)
            if n == 2:
                nc.vector.quantize_mx(out=v_codes[:].bitcast(FP8X4), scales=v_scales[:], in_=v_grouped[:])

        a, y, z = NT - 3, NT - 2, NT - 1
        last = small.tile([P, 4], F32, name="last")
        weighted_sum(a - 1, 0, 8)
        drain_e(a, 0, s_copy)
        drain_e(a, 1, v_copy)
        normalise(a - 1, rinvs[:, a - 1 : a])
        exponentials(z, 0, 1024, last[:, 0:1])
        drain_e(a, 2, v_copy)
        flip_e(y, 0)
        drain_e(a, 3, v_copy)
        flip_e(y, 1)
        flip_e(y, 2)
        flip_e(y, 3)
        exponentials(z, 1024, 2048, last[:, 1:2])
        drain_e(y, 0, v_copy)
        drain_e(y, 1, v_copy)
        flip_e(z, 0)
        flip_e(z, 1)
        quantise_e(a, 0, N)
        exponentials(z, 2048, 3072, last[:, 2:3])
        drain_e(z, 0, s_copy)
        reciprocals(y, y + 1)
        drain_e(y, 2, v_copy)
        weighted_sum(a, 0, 8)
        flip_e(z, 2)
        drain_e(y, 3, v_copy)
        exponentials(z, 3072, 4096, last[:, 3:4])
        drain_e(z, 1, s_copy)
        normalise(a, rinvs[:, a : a + 1])
        quantise_e(y, 0, N)
        flip_e(z, 3)
        drain_e(z, 2, s_copy)
        quantise_e(z, 0, 2048)
        weighted_sum(y, 0, 8)
        drain_e(z, 3, s_copy)
        nc.vector.tensor_reduce(out=rowsums[:, z : z + 1], in_=last[:], axis=mybir.AxisListType.X, op=ALU.add)
        quantise_e(z, 2048, 3072)
        rinv = small.tile([P, 1], F32, name="rinv")
        nc.vector.reciprocal(out=rinv[:], in_=rowsums[:, z : z + 1])
        normalise(y, rinvs[:, y : y + 1])
        weighted_sum(z, 0, 4)
        quantise_e(z, 3072, 4096)
        weighted_sum(z, 4, 8)
        normalise(z, rinv[:])
